import numpy as np
import ml_dtypes


def mxq(x, axis, fmt="e4m3"):
    dtype, down = {"e4m3": (ml_dtypes.float8_e4m3fn, 7), "e5m2": (ml_dtypes.float8_e5m2, 14)}[fmt]
    v = np.moveaxis(np.asarray(x, np.float32).astype(ml_dtypes.bfloat16).astype(np.float64), axis, -1)
    blocks = v.reshape(v.shape[:-1] + (-1, 32))
    amax = np.abs(blocks).max(-1, keepdims=True)
    byte = np.maximum(np.where(amax > 0, np.frexp(amax)[1] - 1 + 127, 0) - down, 1)
    scale = np.exp2(byte - 127.0)
    codes = (blocks / scale).astype(np.float32).astype(dtype).astype(np.float64)
    return np.moveaxis((codes * scale).reshape(v.shape), -1, axis)


WIDE = False


def mx_kscale(k):
    if not WIDE:
        return np.ones(k)
    levels = np.array([10, -10, 5, -5, 0])
    if k % 512:
        return np.exp2(np.random.permutation(np.resize(levels, k // 32))).repeat(32)
    a = np.empty((k // 512, 16))
    for p in range(k // 512):
        a[p, :8] = np.random.permutation(np.resize(levels, 8))
        for g in range(8):
            far = levels[np.abs(levels - a[p, g]) >= 10]
            a[p, g + 8] = far[np.random.randint(len(far))]
    return np.exp2(a.ravel()).repeat(32)


BF16 = ml_dtypes.bfloat16


def bf(x):
    return np.asarray(x, np.float32).astype(BF16)


def f64(x):
    return np.asarray(x).astype(np.float64)


B, N, DIM, H, HKV, D, CACHE, WINDOW = 1, 512, 2048, 16, 4, 128, 1536, 1024
EPS = 1e-6
THETA = 10000.0
HALF = D // 2


def rms_norm(t, w):
    return t * (1.0 / np.sqrt(np.mean(t * t, axis=-1, keepdims=True) + EPS)) * w


def rope(t, cos, sin):
    t2 = t.reshape(*t.shape[:-1], HALF, 2)
    x0, x1 = t2[..., 0], t2[..., 1]
    c = cos[None, None, :, :]
    s = sin[None, None, :, :]
    r0 = x0 * c - x1 * s
    r1 = x0 * s + x1 * c
    return np.stack([r0, r1], axis=-1).reshape(t.shape)


def draw0():
    s = mx_kscale(DIM)
    ang = np.arange(CACHE, CACHE + N)[:, None] * (1.0 / THETA ** (np.arange(0, D, 2) / D))[None, :]
    return {"x": bf(np.random.standard_normal((B, N, DIM)) * s),
            "freqs_cos": bf(np.cos(ang)), "freqs_sin": bf(np.sin(ang)),
            "Wq": bf(np.random.standard_normal((H * D, DIM)) / np.sqrt(DIM) / s[None, :]),
            "Wk": bf(np.random.standard_normal((HKV * D, DIM)) / np.sqrt(DIM) / s[None, :]),
            "Wv": bf(np.random.standard_normal((HKV * D, DIM)) / np.sqrt(DIM) / s[None, :]),
            "wq_norm": bf(2.0 + 0.2 * np.random.standard_normal(D)),
            "wk_norm": bf(1.0 + 0.1 * np.random.standard_normal(D))}


def core(x, freqs_cos, freqs_sin, Wq, Wk, Wv, wq_norm, wk_norm):
    xq = mxq(f64(x), 2, "e4m3")
    q = (xq @ mxq(f64(Wq), 1, "e4m3").T).reshape(B, N, H, D).transpose(0, 2, 1, 3)
    k = (xq @ mxq(f64(Wk), 1, "e4m3").T).reshape(B, N, HKV, D).transpose(0, 2, 1, 3)
    v = (xq @ mxq(f64(Wv), 1, "e4m3").T).reshape(B, N, HKV, D).transpose(0, 2, 1, 3)
    q = rms_norm(q, f64(wq_norm))
    k = rms_norm(k, f64(wk_norm))
    q = rope(q, f64(freqs_cos), f64(freqs_sin))
    k = rope(k, f64(freqs_cos), f64(freqs_sin))
    return q, k, v


def e4m3fn_bytes(y):
    return np.clip(np.asarray(y, np.float64), -448.0, 448.0).astype(np.float32).astype(ml_dtypes.float8_e4m3fn).view(np.uint8)


def e4m3fn_values(b):
    return np.asarray(b, np.uint8).view(ml_dtypes.float8_e4m3fn).astype(np.float64)


def setup_inputs():
    d = draw0()
    x0 = np.asarray(d['Wq']).astype(np.float64)
    s = (np.max(np.abs(x0), axis=(0,), keepdims=True) / 448.0).astype(np.float32)
    out = {}
    for k, v in d.items():
        if k == 'Wq':
            out['Wq_bytes'] = e4m3fn_bytes(x0 / s.astype(np.float64))
            out['Wq_scale'] = s
        else:
            out[k] = v
    return out


def reference(x, freqs_cos, freqs_sin, Wq_bytes, Wq_scale, Wk, Wv, wq_norm, wk_norm):
    return core(x, freqs_cos, freqs_sin, e4m3fn_values(Wq_bytes) * Wq_scale.astype(np.float64), Wk, Wv, wq_norm, wk_norm)

@@ -1,0 +1,286 @@
+from contextlib import ExitStack
+
+import concourse.mybir as mybir
+from concourse.masks import make_identity
+
+F32 = mybir.dt.float32
+BF16 = mybir.dt.bfloat16
+U32 = mybir.dt.uint32
+U8 = mybir.dt.uint8
+FP8 = mybir.dt.float8_e4m3fn
+FP8X4 = mybir.dt.float8_e4m3fn_x4
+ALU = mybir.AluOpType
+ACT = mybir.ActivationFunctionType
+
+P = 128
+K = 2048
+PASSES = 4
+MT = 4
+D = 128
+EPS = 1e-6
+
+FLOPS = 2 * 512 * 2048 * 3072
+
+
+def tile_slidingcacheattention_pa_kernel(
+    tc, x, freqs_cos, freqs_sin, Wq_bytes, Wq_scale, Wk, Wv, wq_norm, wk_norm, out_0, out_1, out_2
+):
+    nc = tc.nc
+    with ExitStack() as ctx:
+        const = ctx.enter_context(tc.tile_pool(name="const", bufs=1))
+        rows = ctx.enter_context(tc.tile_pool(name="rows", bufs=1))
+        deq = ctx.enter_context(tc.tile_pool(name="deq", bufs=8))
+        grp = ctx.enter_context(tc.tile_pool(name="grp", bufs=4))
+        epi = ctx.enter_context(tc.tile_pool(name="epi", bufs=2))
+        tpp = ctx.enter_context(tc.psum_pool(name="tpp", bufs=4))
+        accp = ctx.enter_context(tc.psum_pool(name="accp", bufs=4))
+
+        cos_sb = const.tile([P, MT, 64], BF16, name="cos_sb")
+        sin_sb = const.tile([P, MT, 64], BF16, name="sin_sb")
+        wq_bc = const.tile([P, D], BF16, name="wq_bc")
+        wk_bc = const.tile([P, D], BF16, name="wk_bc")
+        scale_bc = const.tile([P, K], F32, name="scale_bc")
+        wq_view = Wq_bytes.rearrange("(c r p) k -> c p r k", p=P, r=4)
+        qbytes = []
+
+        def load_bytes(c, pieces):
+            qb = rows.tile([P, 4, K], U8, name="qbytes%d" % (c % 2))
+            for a, b in pieces:
+                nc.sync.dma_start(out=qb[:, a:b, :], in_=wq_view[c][:, a:b, :])
+            qbytes.append(qb)
+
+        srow = grp.tile([P, 4, 512], F32, name="grouped", align_bytes=64)
+        for j in range(4):
+            nc.vector.memset(srow[:, j, :], 0.0)
+            nc.sync.dma_start(out=srow[0:1, j, :], in_=Wq_scale[:, 512 * j : 512 * (j + 1)])
+
+        def load_bf16(src, nm):
+            view = src.rearrange("(r p) k -> p r k", p=P)
+            tiles = []
+            for r in range(4):
+                t = rows.tile([P, K], BF16, name="%s%d" % (nm, r))
+                nc.sync.dma_start(out=t[:], in_=view[:, r, :])
+                tiles.append(t)
+            return tiles
+
+        nc.sync.dma_start(out=cos_sb[:], in_=freqs_cos.rearrange("(m p) i -> p m i", p=P))
+        nc.sync.dma_start(out=sin_sb[:], in_=freqs_sin.rearrange("(m p) i -> p m i", p=P))
+        nc.sync.dma_start(out=wq_bc[:], in_=wq_norm.partition_broadcast(P))
+        nc.sync.dma_start(out=wk_bc[:], in_=wk_norm.partition_broadcast(P))
+        load_bytes(0, [(0, 2), (2, 4)])
+        x_sb = load_bf16(x[0], "xv_sb")
+        load_bytes(1, [(0, 4)])
+        wk_sb = load_bf16(Wk, "wk_sb")
+
+        one = const.tile([P, 1], F32, name="one")
+        nc.vector.memset(one[:], 1.0)
+        eps_t = const.tile([P, 1], F32, name="eps_t")
+        nc.vector.memset(eps_t[:], EPS)
+        warm = const.tile([P, 1], F32, name="warm")
+        nc.scalar.activation(out=warm[:], in_=one[:], func=ACT.Sqrt)
+
+        ones = const.tile([P, P], F32, name="ones")
+        nc.gpsimd.memset(ones[:], 1.0)
+        for j in range(4):
+            sp = tpp.tile([P, 512], F32, name="tp")
+            nc.tensor.matmul(out=sp[:], lhsT=ones[:], rhs=srow[:, j, :], start=True, stop=True)
+            nc.scalar.copy(out=scale_bc[:, 512 * j : 512 * (j + 1)], in_=sp[:])
+
+        ident = const.tile([P, P], F32, name="ident")
+        make_identity(nc, ident[:])
+
+        ssg = const.tile([P, MT, 64, 2], BF16, name="ssg")
+        nc.vector.tensor_copy(out=ssg[:, :, :, 0], in_=sin_sb[:])
+        nc.vector.tensor_scalar_mul(out=ssg[:, :, :, 1], in0=sin_sb[:], scalar1=-1.0)
+        tabs = {}
+        for nm, wbc in (("q", wq_bc), ("k", wk_bc)):
+            w4 = wbc[:].rearrange("p (i e) -> p i e", e=2).unsqueeze(1).to_broadcast([P, MT, 64, 2])
+            tab = const.tile([P, MT, 2, D], F32, name="tab_" + nm)
+            nc.vector.tensor_tensor(
+                out=tab[:, :, 0, :].rearrange("p m (i e) -> p m i e", e=2),
+                in0=cos_sb[:].unsqueeze(3).to_broadcast([P, MT, 64, 2]),
+                in1=w4,
+                op=ALU.mult,
+            )
+            nc.vector.tensor_tensor(
+                out=tab[:, :, 1, :].rearrange("p m (i e) -> p m i e", e=2), in0=ssg[:], in1=w4, op=ALU.mult
+            )
+            tabs[nm] = tab
+
+        def mx_tiles(nm):
+            codes = const.tile([P, 4, 512], U32, name="codes_" + nm, align_bytes=64)
+            scl = const.tile([P, 4, 512], U8, name="scl_" + nm, align_bytes=64)
+            return codes, scl
+
+        def dequant(c):
+            tiles = []
+            for r in range(4):
+                t = deq.tile([P, K], BF16, name="wq_bf", align_bytes=64)
+                tiles.append(t)
+            width = 512 if c == 0 else K
+            for k0 in range(0, K, width):
+                for r in range(4):
+                    nc.vector.tensor_tensor(
+                        out=tiles[r][:, k0 : k0 + width],
+                        in0=qbytes[c][:, r, k0 : k0 + width].bitcast(FP8),
+                        in1=scale_bc[:, k0 : k0 + width],
+                        op=ALU.mult,
+                    )
+            if c + 2 < 4:
+                load_bytes(c + 2, [(0, 4)])
+            return tiles
+
+        def turn_quantize(blocks, mx, j):
+            grouped = grp.tile([P, 1024, 4], BF16, name="grouped", align_bytes=64)
+            for b in range(4):
+                tp = tpp.tile([P, 2, 256], F32, name="tp")
+                for r2 in range(2):
+                    t, g = blocks[2 * b + r2]
+                    words = t[:].bitcast(F32)
+                    for u in range(2):
+                        nc.tensor.transpose(
+                            tp[:, u, 128 * r2 : 128 * (r2 + 1)], words[:, 256 * g + u : 256 * (g + 1) : 2], ident[:]
+                        )
+                nc.scalar.copy(
+                    out=grouped[:, 256 * b : 256 * (b + 1), :].bitcast(F32), in_=tp[:].rearrange("p u c -> p c u")
+                )
+            return grouped
+
+        def quantize(grouped, mx, j):
+            nc.vector.quantize_mx(
+                out=mx[0][:, j : j + 2, :].rearrange("p j c -> p (j c)").bitcast(FP8X4),
+                scales=mx[1][:, j : j + 2, :].rearrange("p j c -> p (j c)"),
+                in_=grouped[:].rearrange("p c t -> p (c t)"),
+            )
+
+        def prepare_w(tiles, nm):
+            mx = mx_tiles(nm)
+            gs = [turn_quantize([(tiles[r], g + a) for a in range(2) for r in range(4)], mx, g) for g in (0, 2)]
+            return mx, gs
+
+        def multiply(wmx, m):
+            acc = accp.tile([P, 512], F32, name="acc")
+            for g in range(PASSES):
+                tok = slice(128 * g, 128 * (g + 1))
+                nc.tensor.matmul_mx(
+                    out=acc[:],
+                    lhsT=xmx[0][:, m, tok].bitcast(FP8X4),
+                    lhsT_scale=xmx[1][:, m, tok],
+                    rhs=wmx[0][:, g, :].bitcast(FP8X4),
+                    rhs_scale=wmx[1][:, g, :],
+                    start=(g == 0),
+                    stop=(g == PASSES - 1),
+                )
+            return acc
+
+        def rope_a(st, m):
+            acc = st["acc"][m]
+            for h in range(4):
+                junk = epi.tile([P, D], BF16, name="junk")
+                nc.scalar.activation(
+                    out=junk[:],
+                    in_=acc[:, 128 * h : 128 * (h + 1)],
+                    func=ACT.Square,
+                    accum_out=st["ss"][:, 4 * m + h : 4 * m + h + 1],
+                )
+            mm = epi.tile([P, 2, 4, D], F32, name="mm", bufs=3)
+            nc.vector.tensor_tensor(
+                out=mm[:],
+                in0=acc[:].rearrange("p (h d) -> p h d", h=4).unsqueeze(1).to_broadcast([P, 2, 4, D]),
+                in1=tabs[st["nm"]][:, m, :, :].unsqueeze(2).to_broadcast([P, 2, 4, D]),
+                op=ALU.mult,
+            )
+            r = epi.tile([P, 4, D], F32, name="r", bufs=8)
+            st["r"].append(r)
+            if m < 3:
+                pair_sum(nc.gpsimd, r, mm)
+            else:
+                st["late"] = mm
+
+        def pair_sum(eng, r, mm):
+            eng.tensor_tensor(
+                out=r[:].rearrange("p h (i e) -> p (h i) e", e=2),
+                in0=mm[:, 0, :, :].rearrange("p h (i e) -> p (h i) e", e=2),
+                in1=mm[:, 1, :, :].rearrange("p h (i e) -> p (h i) e", e=2)[:, :, ::-1],
+                op=ALU.add,
+            )
+
+        def rope_b(st):
+            std = epi.tile([P, 16], F32, name="std")
+            rstd = epi.tile([P, 16], F32, name="rstd")
+            nc.scalar.activation(out=std[:], in_=st["ss"][:], func=ACT.Sqrt, bias=eps_t[:], scale=1.0 / D)
+            nc.vector.reciprocal(out=rstd[:], in_=std[:])
+            pair_sum(nc.vector, st["r"][3], st["late"])
+            for m in range(MT):
+                r = st["r"][m]
+                for h in range(4):
+                    nc.scalar.activation(
+                        out=r[:, h, :], in_=r[:, h, :], func=ACT.Copy, scale=rstd[:, 4 * m + h : 4 * m + h + 1]
+                    )
+                nc.sync.dma_start(
+                    out=st["dst"][:, 128 * m : 128 * (m + 1), :].rearrange("h n d -> n h d"), in_=r[:]
+                )
+
+        def rope_c(st, m):
+            std = epi.tile([P, 4], F32, name="std4", bufs=4)
+            rstd = epi.tile([P, 4], F32, name="rstd4", bufs=4)
+            nc.scalar.activation(
+                out=std[:], in_=st["ss"][:, 4 * m : 4 * m + 4], func=ACT.Sqrt, bias=eps_t[:], scale=1.0 / D
+            )
+            nc.vector.reciprocal(out=rstd[:], in_=std[:])
+            r = st["r"][m]
+            for h in range(4):
+                nc.scalar.activation(out=r[:, h, :], in_=r[:, h, :], func=ACT.Copy, scale=rstd[:, h : h + 1])
+            nc.sync.dma_start(out=st["dst"][:, 128 * m : 128 * (m + 1), :].rearrange("h n d -> n h d"), in_=r[:])
+
+        def plain_out(st, m):
+            vsb = epi.tile([P, 4, D], F32, name="r", bufs=8)
+            nc.scalar.copy(out=vsb[:].rearrange("p h d -> p (h d)"), in_=st["acc"][m][:])
+            nc.sync.dma_start(out=st["dst"][:, 128 * m : 128 * (m + 1), :].rearrange("h n d -> n h d"), in_=vsb[:])
+
+        def finish(st, m):
+            if st["nm"] == "v":
+                plain_out(st, m)
+            else:
+                rope_a(st, m)
+
+        q_bf = {0: dequant(0)}
+        xmx = mx_tiles("x")
+        for m in (0, 2):
+            quantize(turn_quantize([(x_sb[m + a], g) for a in range(2) for g in range(PASSES)], xmx, m), xmx, m)
+        wv_sb = load_bf16(Wv, "xv_sb")
+
+        order = [("q", 0), ("k", 0), ("q", 1), ("q", 2), ("v", 0), ("q", 3)]
+        next_q = 1
+        prev = None
+        for nm, c in order:
+            if nm == "q":
+                wmx, gs = prepare_w(q_bf[c], "q%d" % c)
+                dst = out_0[0, 4 * c : 4 * (c + 1), :, :]
+            elif nm == "k":
+                wmx, gs = prepare_w(wk_sb, "k")
+                dst = out_1[0]
+            else:
+                wmx, gs = prepare_w(wv_sb, "v")
+                dst = out_2[0]
+            if nm == "q" and next_q < 4:
+                q_bf[next_q] = dequant(next_q)
+                next_q += 1
+            quantize(gs[0], wmx, 0)
+            quantize(gs[1], wmx, 2)
+            st = {"nm": nm, "dst": dst, "acc": [], "r": []}
+            if nm != "v":
+                ss = epi.tile([P, 16], F32, name="ss")
+                st["ss"] = ss
+            for m in range(MT):
+                if prev is not None:
+                    finish(prev, m)
+                st["acc"].append(multiply(wmx, m))
+            if prev is not None and prev["nm"] != "v":
+                rope_b(prev)
+            prev = st
+        for m in range(MT):
+            rope_a(prev, m)
+            if m == 3:
+                pair_sum(nc.vector, prev["r"][3], prev["late"])
+            rope_c(prev, m)

@@ -77,7 +77,7 @@ def tile_slidingcacheattention_pa_kernel(
         eps_t = const.tile([P, 1], F32, name="eps_t")
         nc.vector.memset(eps_t[:], EPS)
         warm = const.tile([P, 1], F32, name="warm")
-        nc.scalar.activation(out=warm[:], in_=one[:], func=ACT.Sqrt)
+        nc.scalar.activation(out=warm[:], in_=one[:], func=ACT.Abs_reciprocal_sqrt)
 
         ones = const.tile([P, P], F32, name="ones")
         nc.gpsimd.memset(ones[:], 1.0)
@@ -175,6 +175,13 @@ def tile_slidingcacheattention_pa_kernel(
 
         def rope_a(st, m):
             acc = st["acc"][m]
+            mm = epi.tile([P, 2, 4, D], F32, name="mm", bufs=3)
+            nc.vector.tensor_tensor(
+                out=mm[:],
+                in0=acc[:].rearrange("p (h d) -> p h d", h=4).unsqueeze(1).to_broadcast([P, 2, 4, D]),
+                in1=tabs[st["nm"]][:, m, :, :].unsqueeze(2).to_broadcast([P, 2, 4, D]),
+                op=ALU.mult,
+            )
             for h in range(4):
                 junk = epi.tile([P, D], BF16, name="junk")
                 nc.scalar.activation(
@@ -183,13 +190,6 @@ def tile_slidingcacheattention_pa_kernel(
                     func=ACT.Square,
                     accum_out=st["ss"][:, 4 * m + h : 4 * m + h + 1],
                 )
-            mm = epi.tile([P, 2, 4, D], F32, name="mm", bufs=3)
-            nc.vector.tensor_tensor(
-                out=mm[:],
-                in0=acc[:].rearrange("p (h d) -> p h d", h=4).unsqueeze(1).to_broadcast([P, 2, 4, D]),
-                in1=tabs[st["nm"]][:, m, :, :].unsqueeze(2).to_broadcast([P, 2, 4, D]),
-                op=ALU.mult,
-            )
             r = epi.tile([P, 4, D], F32, name="r", bufs=8)
             st["r"].append(r)
             if m < 3:
@@ -206,10 +206,10 @@ def tile_slidingcacheattention_pa_kernel(
             )
 
         def rope_b(st):
-            std = epi.tile([P, 16], F32, name="std")
             rstd = epi.tile([P, 16], F32, name="rstd")
-            nc.scalar.activation(out=std[:], in_=st["ss"][:], func=ACT.Sqrt, bias=eps_t[:], scale=1.0 / D)
-            nc.vector.reciprocal(out=rstd[:], in_=std[:])
+            nc.scalar.activation(
+                out=rstd[:], in_=st["ss"][:], func=ACT.Abs_reciprocal_sqrt, bias=eps_t[:], scale=1.0 / D
+            )
             pair_sum(nc.vector, st["r"][3], st["late"])
             for m in range(MT):
                 r = st["r"][m]
@@ -222,12 +222,14 @@ def tile_slidingcacheattention_pa_kernel(
                 )
 
         def rope_c(st, m):
-            std = epi.tile([P, 4], F32, name="std4", bufs=4)
             rstd = epi.tile([P, 4], F32, name="rstd4", bufs=4)
             nc.scalar.activation(
-                out=std[:], in_=st["ss"][:, 4 * m : 4 * m + 4], func=ACT.Sqrt, bias=eps_t[:], scale=1.0 / D
+                out=rstd[:],
+                in_=st["ss"][:, 4 * m : 4 * m + 4],
+                func=ACT.Abs_reciprocal_sqrt,
+                bias=eps_t[:],
+                scale=1.0 / D,
             )
-            nc.vector.reciprocal(out=rstd[:], in_=std[:])
             r = st["r"][m]
             for h in range(4):
                 nc.scalar.activation(out=r[:, h, :], in_=r[:, h, :], func=ACT.Copy, scale=rstd[:, h : h + 1])

@@ -21,6 +21,19 @@ EPS = 1e-6
 
 FLOPS = 2 * 512 * 2048 * 3072
 
+CFG = {
+    "order": [("q", 0), ("k", 0), ("q", 1), ("q", 2), ("v", 0), ("q", 3)],
+    "gsum": 2,
+    "gsum_last": 2,
+    "vscale_last": 0,
+    "per_tile": False,
+    "tp": 4,
+    "acc": 4,
+    "mm": 3,
+    "r": 8,
+    "d_late": False,
+}
+
 
 def tile_slidingcacheattention_pa_kernel(
     tc, x, freqs_cos, freqs_sin, Wq_bytes, Wq_scale, Wk, Wv, wq_norm, wk_norm, out_0, out_1, out_2
@@ -32,8 +45,8 @@ def tile_slidingcacheattention_pa_kernel(
         deq = ctx.enter_context(tc.tile_pool(name="deq", bufs=8))
         grp = ctx.enter_context(tc.tile_pool(name="grp", bufs=4))
         epi = ctx.enter_context(tc.tile_pool(name="epi", bufs=2))
-        tpp = ctx.enter_context(tc.psum_pool(name="tpp", bufs=4))
-        accp = ctx.enter_context(tc.psum_pool(name="accp", bufs=4))
+        tpp = ctx.enter_context(tc.psum_pool(name="tpp", bufs=CFG["tp"]))
+        accp = ctx.enter_context(tc.psum_pool(name="accp", bufs=CFG["acc"]))
 
         cos_sb = const.tile([P, MT, 64], BF16, name="cos_sb")
         sin_sb = const.tile([P, MT, 64], BF16, name="sin_sb")
@@ -175,7 +188,7 @@ def tile_slidingcacheattention_pa_kernel(
 
         def rope_a(st, m):
             acc = st["acc"][m]
-            mm = epi.tile([P, 2, 4, D], F32, name="mm", bufs=3)
+            mm = epi.tile([P, 2, 4, D], F32, name="mm", bufs=CFG["mm"])
             nc.vector.tensor_tensor(
                 out=mm[:],
                 in0=acc[:].rearrange("p (h d) -> p h d", h=4).unsqueeze(1).to_broadcast([P, 2, 4, D]),
@@ -190,12 +203,14 @@ def tile_slidingcacheattention_pa_kernel(
                     func=ACT.Square,
                     accum_out=st["ss"][:, 4 * m + h : 4 * m + h + 1],
                 )
-            r = epi.tile([P, 4, D], F32, name="r", bufs=8)
+            r = epi.tile([P, 4, D], F32, name="r", bufs=CFG["r"])
             st["r"].append(r)
-            if m < 3:
+            if m < st["gsum"]:
                 pair_sum(nc.gpsimd, r, mm)
+            elif st["fine"]:
+                pair_sum(nc.vector, r, mm)
             else:
-                st["late"] = mm
+                st["late"].append((r, mm))
 
         def pair_sum(eng, r, mm):
             eng.tensor_tensor(
@@ -210,7 +225,8 @@ def tile_slidingcacheattention_pa_kernel(
             nc.scalar.activation(
                 out=rstd[:], in_=st["ss"][:], func=ACT.Abs_reciprocal_sqrt, bias=eps_t[:], scale=1.0 / D
             )
-            pair_sum(nc.vector, st["r"][3], st["late"])
+            for r, mm in st["late"]:
+                pair_sum(nc.vector, r, mm)
             for m in range(MT):
                 r = st["r"][m]
                 for h in range(4):
@@ -232,11 +248,14 @@ def tile_slidingcacheattention_pa_kernel(
             )
             r = st["r"][m]
             for h in range(4):
-                nc.scalar.activation(out=r[:, h, :], in_=r[:, h, :], func=ACT.Copy, scale=rstd[:, h : h + 1])
+                if m >= MT - st["vscale"]:
+                    nc.vector.tensor_scalar_mul(out=r[:, h, :], in0=r[:, h, :], scalar1=rstd[:, h : h + 1])
+                else:
+                    nc.scalar.activation(out=r[:, h, :], in_=r[:, h, :], func=ACT.Copy, scale=rstd[:, h : h + 1])
             nc.sync.dma_start(out=st["dst"][:, 128 * m : 128 * (m + 1), :].rearrange("h n d -> n h d"), in_=r[:])
 
         def plain_out(st, m):
-            vsb = epi.tile([P, 4, D], F32, name="r", bufs=8)
+            vsb = epi.tile([P, 4, D], F32, name="r", bufs=CFG["r"])
             nc.scalar.copy(out=vsb[:].rearrange("p h d -> p (h d)"), in_=st["acc"][m][:])
             nc.sync.dma_start(out=st["dst"][:, 128 * m : 128 * (m + 1), :].rearrange("h n d -> n h d"), in_=vsb[:])
 
@@ -245,6 +264,8 @@ def tile_slidingcacheattention_pa_kernel(
                 plain_out(st, m)
             else:
                 rope_a(st, m)
+                if st["fine"]:
+                    rope_c(st, m)
 
         q_bf = {0: dequant(0)}
         xmx = mx_tiles("x")
@@ -252,10 +273,10 @@ def tile_slidingcacheattention_pa_kernel(
             quantize(turn_quantize([(x_sb[m + a], g) for a in range(2) for g in range(PASSES)], xmx, m), xmx, m)
         wv_sb = load_bf16(Wv, "xv_sb")
 
-        order = [("q", 0), ("k", 0), ("q", 1), ("q", 2), ("v", 0), ("q", 3)]
+        order = CFG["order"]
         next_q = 1
         prev = None
-        for nm, c in order:
+        for i, (nm, c) in enumerate(order):
             if nm == "q":
                 wmx, gs = prepare_w(q_bf[c], "q%d" % c)
                 dst = out_0[0, 4 * c : 4 * (c + 1), :, :]
@@ -265,12 +286,22 @@ def tile_slidingcacheattention_pa_kernel(
             else:
                 wmx, gs = prepare_w(wv_sb, "v")
                 dst = out_2[0]
-            if nm == "q" and next_q < 4:
+            if nm == "q" and next_q < 4 and not CFG["d_late"]:
                 q_bf[next_q] = dequant(next_q)
                 next_q += 1
             quantize(gs[0], wmx, 0)
             quantize(gs[1], wmx, 2)
-            st = {"nm": nm, "dst": dst, "acc": [], "r": []}
+            last = i == len(order) - 1
+            st = {
+                "nm": nm,
+                "dst": dst,
+                "acc": [],
+                "r": [],
+                "late": [],
+                "gsum": CFG["gsum_last"] if last else CFG["gsum"],
+                "fine": last or CFG["per_tile"],
+                "vscale": CFG["vscale_last"] if last else 0,
+            }
             if nm != "v":
                 ss = epi.tile([P, 16], F32, name="ss")
                 st["ss"] = ss
@@ -278,11 +309,11 @@ def tile_slidingcacheattention_pa_kernel(
                 if prev is not None:
                     finish(prev, m)
                 st["acc"].append(multiply(wmx, m))
-            if prev is not None and prev["nm"] != "v":
+            if prev is not None and prev["nm"] != "v" and not prev["fine"]:
                 rope_b(prev)
+            if nm == "q" and next_q < 4 and CFG["d_late"]:
+                q_bf[next_q] = dequant(next_q)
+                next_q += 1
             prev = st
         for m in range(MT):
-            rope_a(prev, m)
-            if m == 3:
-                pair_sum(nc.vector, prev["r"][3], prev["late"])
-            rope_c(prev, m)
+            finish(prev, m)

@@ -23,10 +23,10 @@ FLOPS = 2 * 512 * 2048 * 3072
 
 CFG = {
     "order": [("q", 0), ("k", 0), ("q", 1), ("q", 2), ("v", 0), ("q", 3)],
-    "gsum": 2,
-    "gsum_last": 2,
-    "vscale_last": 0,
-    "per_tile": False,
+    "sums": ["ggpp", "ggpp", "ggvp", "ggvv", "", "ggvv"],
+    "last_tp": False,
+    "vscale": [0, 0, 0, 0, 0, 0],
+    "fine": [False, False, False, False, False, True],
     "tp": 4,
     "acc": 4,
     "mm": 3,
@@ -102,22 +102,19 @@ def tile_slidingcacheattention_pa_kernel(
         ident = const.tile([P, P], F32, name="ident")
         make_identity(nc, ident[:])
 
-        ssg = const.tile([P, MT, 64, 2], BF16, name="ssg")
-        nc.vector.tensor_copy(out=ssg[:, :, :, 0], in_=sin_sb[:])
-        nc.vector.tensor_scalar_mul(out=ssg[:, :, :, 1], in0=sin_sb[:], scalar1=-1.0)
         tabs = {}
         for nm, wbc in (("q", wq_bc), ("k", wk_bc)):
-            w4 = wbc[:].rearrange("p (i e) -> p i e", e=2).unsqueeze(1).to_broadcast([P, MT, 64, 2])
-            tab = const.tile([P, MT, 2, D], F32, name="tab_" + nm)
-            nc.vector.tensor_tensor(
-                out=tab[:, :, 0, :].rearrange("p m (i e) -> p m i e", e=2),
-                in0=cos_sb[:].unsqueeze(3).to_broadcast([P, MT, 64, 2]),
-                in1=w4,
-                op=ALU.mult,
-            )
-            nc.vector.tensor_tensor(
-                out=tab[:, :, 1, :].rearrange("p m (i e) -> p m i e", e=2), in0=ssg[:], in1=w4, op=ALU.mult
-            )
+            tab = const.tile([P, MT, 2, 64, 2], F32, name="tab_" + nm)
+            wj = wbc[:].rearrange("p (i j) -> p j i", j=2)
+            for j, e, src, sign in ((0, 0, cos_sb, 1.0), (0, 1, sin_sb, 1.0), (1, 0, sin_sb, -1.0), (1, 1, cos_sb, 1.0)):
+                nc.vector.scalar_tensor_tensor(
+                    out=tab[:, :, j, :, e],
+                    in0=src[:],
+                    scalar=sign,
+                    in1=wj[:, j, :].unsqueeze(1).to_broadcast([P, MT, 64]),
+                    op0=ALU.mult,
+                    op1=ALU.mult,
+                )
             tabs[nm] = tab
 
         def mx_tiles(nm):
@@ -171,8 +168,8 @@ def tile_slidingcacheattention_pa_kernel(
             gs = [turn_quantize([(tiles[r], g + a) for a in range(2) for r in range(4)], mx, g) for g in (0, 2)]
             return mx, gs
 
-        def multiply(wmx, m):
-            acc = accp.tile([P, 512], F32, name="acc")
+        def multiply(wmx, m, pool, nm):
+            acc = pool.tile([P, 512], F32, name=nm)
             for g in range(PASSES):
                 tok = slice(128 * g, 128 * (g + 1))
                 nc.tensor.matmul_mx(
@@ -188,11 +185,11 @@ def tile_slidingcacheattention_pa_kernel(
 
         def rope_a(st, m):
             acc = st["acc"][m]
-            mm = epi.tile([P, 2, 4, D], F32, name="mm", bufs=CFG["mm"])
+            mm = epi.tile([P, 2, 4, 64, 2], F32, name="mm", bufs=CFG["mm"])
             nc.vector.tensor_tensor(
                 out=mm[:],
-                in0=acc[:].rearrange("p (h d) -> p h d", h=4).unsqueeze(1).to_broadcast([P, 2, 4, D]),
-                in1=tabs[st["nm"]][:, m, :, :].unsqueeze(2).to_broadcast([P, 2, 4, D]),
+                in0=acc[:].rearrange("p (h i j) -> p j h i", h=4, j=2).unsqueeze(4).to_broadcast([P, 2, 4, 64, 2]),
+                in1=tabs[st["nm"]][:, m, :, :, :].unsqueeze(2).to_broadcast([P, 2, 4, 64, 2]),
                 op=ALU.mult,
             )
             for h in range(4):
@@ -205,8 +202,21 @@ def tile_slidingcacheattention_pa_kernel(
                 )
             r = epi.tile([P, 4, D], F32, name="r", bufs=CFG["r"])
             st["r"].append(r)
-            if m < st["gsum"]:
+            who = st["sums"][m]
+            st["src"].append(r)
+            if who == "g":
                 pair_sum(nc.gpsimd, r, mm)
+            elif who == "p":
+                ps = tpp.tile([P, 4, D], F32, name="tp")
+                for j in range(2):
+                    nc.tensor.matmul(
+                        out=ps[:].rearrange("p h d -> p (h d)"),
+                        lhsT=ident[:],
+                        rhs=mm[:, j, :, :, :].rearrange("p h i e -> p (h i e)"),
+                        start=(j == 0),
+                        stop=(j == 1),
+                    )
+                st["src"][m] = ps
             elif st["fine"]:
                 pair_sum(nc.vector, r, mm)
             else:
@@ -214,9 +224,9 @@ def tile_slidingcacheattention_pa_kernel(
 
         def pair_sum(eng, r, mm):
             eng.tensor_tensor(
-                out=r[:].rearrange("p h (i e) -> p (h i) e", e=2),
-                in0=mm[:, 0, :, :].rearrange("p h (i e) -> p (h i) e", e=2),
-                in1=mm[:, 1, :, :].rearrange("p h (i e) -> p (h i) e", e=2)[:, :, ::-1],
+                out=r[:].rearrange("p h d -> p (h d)"),
+                in0=mm[:, 0, :, :, :].rearrange("p h i e -> p (h i e)"),
+                in1=mm[:, 1, :, :, :].rearrange("p h i e -> p (h i e)"),
                 op=ALU.add,
             )
 
@@ -230,9 +240,17 @@ def tile_slidingcacheattention_pa_kernel(
             for m in range(MT):
                 r = st["r"][m]
                 for h in range(4):
-                    nc.scalar.activation(
-                        out=r[:, h, :], in_=r[:, h, :], func=ACT.Copy, scale=rstd[:, 4 * m + h : 4 * m + h + 1]
-                    )
+                    if m >= MT - st["vscale"]:
+                        nc.vector.tensor_scalar_mul(
+                            out=r[:, h, :], in0=st["src"][m][:, h, :], scalar1=rstd[:, 4 * m + h : 4 * m + h + 1]
+                        )
+                    else:
+                        nc.scalar.activation(
+                            out=r[:, h, :],
+                            in_=st["src"][m][:, h, :],
+                            func=ACT.Copy,
+                            scale=rstd[:, 4 * m + h : 4 * m + h + 1],
+                        )
                 nc.sync.dma_start(
                     out=st["dst"][:, 128 * m : 128 * (m + 1), :].rearrange("h n d -> n h d"), in_=r[:]
                 )
@@ -249,9 +267,11 @@ def tile_slidingcacheattention_pa_kernel(
             r = st["r"][m]
             for h in range(4):
                 if m >= MT - st["vscale"]:
-                    nc.vector.tensor_scalar_mul(out=r[:, h, :], in0=r[:, h, :], scalar1=rstd[:, h : h + 1])
+                    nc.vector.tensor_scalar_mul(out=r[:, h, :], in0=st["src"][m][:, h, :], scalar1=rstd[:, h : h + 1])
                 else:
-                    nc.scalar.activation(out=r[:, h, :], in_=r[:, h, :], func=ACT.Copy, scale=rstd[:, h : h + 1])
+                    nc.scalar.activation(
+                        out=r[:, h, :], in_=st["src"][m][:, h, :], func=ACT.Copy, scale=rstd[:, h : h + 1]
+                    )
             nc.sync.dma_start(out=st["dst"][:, 128 * m : 128 * (m + 1), :].rearrange("h n d -> n h d"), in_=r[:])
 
         def plain_out(st, m):
@@ -298,9 +318,10 @@ def tile_slidingcacheattention_pa_kernel(
                 "acc": [],
                 "r": [],
                 "late": [],
-                "gsum": CFG["gsum_last"] if last else CFG["gsum"],
-                "fine": last or CFG["per_tile"],
-                "vscale": CFG["vscale_last"] if last else 0,
+                "src": [],
+                "sums": CFG["sums"][i],
+                "fine": CFG["fine"][i],
+                "vscale": CFG["vscale"][i],
             }
             if nm != "v":
                 ss = epi.tile([P, 16], F32, name="ss")
@@ -308,7 +329,10 @@ def tile_slidingcacheattention_pa_kernel(
             for m in range(MT):
                 if prev is not None:
                     finish(prev, m)
-                st["acc"].append(multiply(wmx, m))
+                if last and CFG["last_tp"]:
+                    st["acc"].append(multiply(wmx, m, tpp, "tp"))
+                else:
+                    st["acc"].append(multiply(wmx, m, accp, "acc"))
             if prev is not None and prev["nm"] != "v" and not prev["fine"]:
                 rope_b(prev)
             if nm == "q" and next_q < 4 and CFG["d_late"]:

@@ -23,11 +23,12 @@ FLOPS = 2 * 512 * 2048 * 3072
 
 CFG = {
     "order": [("q", 0), ("k", 0), ("q", 1), ("q", 2), ("v", 0), ("q", 3)],
-    "sums": ["ggpp", "ggpp", "ggvp", "ggvv", "", "ggvv"],
+    "sums": ["ggvp", "ggvp", "ggvp", "ggvv", "", "ggvv"],
     "last_tp": False,
     "vscale": [0, 0, 0, 0, 0, 0],
     "fine": [False, False, False, False, False, True],
-    "tp": 4,
+    "tp": 3,
+    "ps": 1,
     "acc": 4,
     "mm": 3,
     "r": 8,
@@ -47,6 +48,7 @@ def tile_slidingcacheattention_pa_kernel(
         epi = ctx.enter_context(tc.tile_pool(name="epi", bufs=2))
         tpp = ctx.enter_context(tc.psum_pool(name="tpp", bufs=CFG["tp"]))
         accp = ctx.enter_context(tc.psum_pool(name="accp", bufs=CFG["acc"]))
+        psp = ctx.enter_context(tc.psum_pool(name="psp", bufs=CFG["ps"])) if CFG["ps"] else tpp
 
         cos_sb = const.tile([P, MT, 64], BF16, name="cos_sb")
         sin_sb = const.tile([P, MT, 64], BF16, name="sin_sb")
@@ -102,18 +104,19 @@ def tile_slidingcacheattention_pa_kernel(
         ident = const.tile([P, P], F32, name="ident")
         make_identity(nc, ident[:])
 
+        cs4 = const.tile([P, MT, 2, 64, 2], BF16, name="cs4")
+        for j, e, src, sign in ((0, 0, cos_sb, 1.0), (0, 1, sin_sb, 1.0), (1, 0, sin_sb, -1.0), (1, 1, cos_sb, 1.0)):
+            nc.scalar.activation(out=cs4[:, :, j, :, e], in_=src[:], func=ACT.Copy, scale=sign)
         tabs = {}
         for nm, wbc in (("q", wq_bc), ("k", wk_bc)):
             tab = const.tile([P, MT, 2, 64, 2], F32, name="tab_" + nm)
             wj = wbc[:].rearrange("p (i j) -> p j i", j=2)
-            for j, e, src, sign in ((0, 0, cos_sb, 1.0), (0, 1, sin_sb, 1.0), (1, 0, sin_sb, -1.0), (1, 1, cos_sb, 1.0)):
-                nc.vector.scalar_tensor_tensor(
-                    out=tab[:, :, j, :, e],
-                    in0=src[:],
-                    scalar=sign,
-                    in1=wj[:, j, :].unsqueeze(1).to_broadcast([P, MT, 64]),
-                    op0=ALU.mult,
-                    op1=ALU.mult,
+            for j in range(2):
+                nc.vector.tensor_tensor(
+                    out=tab[:, :, j, :, :],
+                    in0=cs4[:, :, j, :, :],
+                    in1=wj[:, j, :].unsqueeze(1).unsqueeze(3).to_broadcast([P, MT, 64, 2]),
+                    op=ALU.mult,
                 )
             tabs[nm] = tab
 
@@ -207,7 +210,7 @@ def tile_slidingcacheattention_pa_kernel(
             if who == "g":
                 pair_sum(nc.gpsimd, r, mm)
             elif who == "p":
-                ps = tpp.tile([P, 4, D], F32, name="tp")
+                ps = psp.tile([P, 4, D], F32, name="ps" if CFG["ps"] else "tp")
                 for j in range(2):
                     nc.tensor.matmul(
                         out=ps[:].rearrange("p h d -> p (h d)"),

@@ -23,12 +23,12 @@ FLOPS = 2 * 512 * 2048 * 3072
 
 CFG = {
     "order": [("q", 0), ("k", 0), ("q", 1), ("q", 2), ("v", 0), ("q", 3)],
-    "sums": ["ggvp", "ggvp", "ggvp", "ggvv", "", "ggvv"],
+    "sums": ["ggvv", "ggvv", "ggvv", "ggvv", "", "ggvv"],
     "last_tp": False,
     "vscale": [0, 0, 0, 0, 0, 0],
     "fine": [False, False, False, False, False, True],
-    "tp": 3,
-    "ps": 1,
+    "tp": 4,
+    "ps": 0,
     "acc": 4,
     "mm": 3,
     "r": 8,

@@ -28,11 +28,15 @@ CFG = {
     "vscale": [0, 0, 0, 0, 0, 0],
     "fine": [False, False, False, False, False, True],
     "tp": 4,
+    "d0": [512, 512, 1024],
     "ps": 0,
+    "ps_acc": False,
     "acc": 4,
     "mm": 3,
     "r": 8,
     "d_late": False,
+    "qx_late": False,
+    "q_late": [False] * 6,
 }
 
 
@@ -50,24 +54,20 @@ def tile_slidingcacheattention_pa_kernel(
         accp = ctx.enter_context(tc.psum_pool(name="accp", bufs=CFG["acc"]))
         psp = ctx.enter_context(tc.psum_pool(name="psp", bufs=CFG["ps"])) if CFG["ps"] else tpp
 
-        cos_sb = const.tile([P, MT, 64], BF16, name="cos_sb")
-        sin_sb = const.tile([P, MT, 64], BF16, name="sin_sb")
-        wq_bc = const.tile([P, D], BF16, name="wq_bc")
-        wk_bc = const.tile([P, D], BF16, name="wk_bc")
         scale_bc = const.tile([P, K], F32, name="scale_bc")
         wq_view = Wq_bytes.rearrange("(c r p) k -> c p r k", p=P, r=4)
         qbytes = []
+
+        def load_scale(j):
+            nc.sync.dma_start(
+                out=scale_bc[:, 512 * j : 512 * (j + 1)], in_=Wq_scale[0, 512 * j : 512 * (j + 1)].partition_broadcast(P)
+            )
 
         def load_bytes(c, pieces):
             qb = rows.tile([P, 4, K], U8, name="qbytes%d" % (c % 2))
             for a, b in pieces:
                 nc.sync.dma_start(out=qb[:, a:b, :], in_=wq_view[c][:, a:b, :])
             qbytes.append(qb)
-
-        srow = grp.tile([P, 4, 512], F32, name="grouped", align_bytes=64)
-        for j in range(4):
-            nc.vector.memset(srow[:, j, :], 0.0)
-            nc.sync.dma_start(out=srow[0:1, j, :], in_=Wq_scale[:, 512 * j : 512 * (j + 1)])
 
         def load_bf16(src, nm):
             view = src.rearrange("(r p) k -> p r k", p=P)
@@ -78,11 +78,19 @@ def tile_slidingcacheattention_pa_kernel(
                 tiles.append(t)
             return tiles
 
-        nc.sync.dma_start(out=cos_sb[:], in_=freqs_cos.rearrange("(m p) i -> p m i", p=P))
-        nc.sync.dma_start(out=sin_sb[:], in_=freqs_sin.rearrange("(m p) i -> p m i", p=P))
-        nc.sync.dma_start(out=wq_bc[:], in_=wq_norm.partition_broadcast(P))
-        nc.sync.dma_start(out=wk_bc[:], in_=wk_norm.partition_broadcast(P))
+        cs_sb = const.tile([P, MT, 2, 64], BF16, name="cs_sb")
+        nc.sync.dma_start(out=cs_sb[:, :, 0, :], in_=freqs_cos.rearrange("(m p) i -> p m i", p=P))
+        nc.sync.dma_start(out=cs_sb[:, :, 1, :], in_=freqs_sin.rearrange("(m p) i -> p m i", p=P))
+        wc_bf = {}
+        for nm, w in (("q", wq_norm), ("k", wk_norm)):
+            t = const.tile([P, 2], BF16, name="wc_bf_" + nm)
+            for half in range(2):
+                nc.sync.dma_start(out=t[64 * half : 64 * (half + 1), :], in_=w.rearrange("(i j) -> i j", j=2))
+            wc_bf[nm] = t
+        load_scale(0)
         load_bytes(0, [(0, 2), (2, 4)])
+        for j in range(1, 4):
+            load_scale(j)
         x_sb = load_bf16(x[0], "xv_sb")
         load_bytes(1, [(0, 4)])
         wk_sb = load_bf16(Wk, "wk_sb")
@@ -93,32 +101,44 @@ def tile_slidingcacheattention_pa_kernel(
         nc.vector.memset(eps_t[:], EPS)
         warm = const.tile([P, 1], F32, name="warm")
         nc.scalar.activation(out=warm[:], in_=one[:], func=ACT.Abs_reciprocal_sqrt)
-
-        ones = const.tile([P, P], F32, name="ones")
-        nc.gpsimd.memset(ones[:], 1.0)
-        for j in range(4):
-            sp = tpp.tile([P, 512], F32, name="tp")
-            nc.tensor.matmul(out=sp[:], lhsT=ones[:], rhs=srow[:, j, :], start=True, stop=True)
-            nc.scalar.copy(out=scale_bc[:, 512 * j : 512 * (j + 1)], in_=sp[:])
-
         ident = const.tile([P, P], F32, name="ident")
         make_identity(nc, ident[:])
+        identb = const.tile([P, P], BF16, name="identb")
+        make_identity(nc, identb[:])
 
-        cs4 = const.tile([P, MT, 2, 64, 2], BF16, name="cs4")
-        for j, e, src, sign in ((0, 0, cos_sb, 1.0), (0, 1, sin_sb, 1.0), (1, 0, sin_sb, -1.0), (1, 1, cos_sb, 1.0)):
-            nc.scalar.activation(out=cs4[:, :, j, :, e], in_=src[:], func=ACT.Copy, scale=sign)
-        tabs = {}
-        for nm, wbc in (("q", wq_bc), ("k", wk_bc)):
-            tab = const.tile([P, MT, 2, 64, 2], F32, name="tab_" + nm)
-            wj = wbc[:].rearrange("p (i j) -> p j i", j=2)
-            for j in range(2):
-                nc.vector.tensor_tensor(
-                    out=tab[:, :, j, :, :],
-                    in0=cs4[:, :, j, :, :],
-                    in1=wj[:, j, :].unsqueeze(1).unsqueeze(3).to_broadcast([P, MT, 64, 2]),
-                    op=ALU.mult,
+        tabs_all = const.tile([P, MT, 2, 2, 64, 2], F32, name="tabs_all")
+
+        def build_tables():
+            cstp = accp.tile([P, MT, P], BF16, name="acc")
+            for m in range(MT):
+                nc.tensor.transpose(cstp[:, m, :], cs_sb[:, m, :, :].rearrange("p c i -> p (c i)"), identb[:])
+            cst = const.tile([P, MT, P], BF16, name="cst")
+            nc.scalar.copy(out=cst[:], in_=cstp[:])
+            sel = const.tile([P, 2, 2, 64, 2], BF16, name="sel")
+            for t, nm in enumerate(("q", "k")):
+                wc = const.tile([P, 3], F32, name="wc_" + nm)
+                nc.scalar.copy(out=wc[:, 0:2], in_=wc_bf[nm][:])
+                nc.scalar.activation(out=wc[:, 2:3], in_=wc_bf[nm][:, 1:2], func=ACT.Copy, scale=-1.0)
+                for j, e, c, col in ((0, 0, 0, 0), (0, 1, 1, 0), (1, 0, 1, 2), (1, 1, 0, 1)):
+                    nc.scalar.activation(
+                        out=sel[:, t, j, :, e],
+                        in_=identb[:, 64 * c : 64 * (c + 1)],
+                        func=ACT.Copy,
+                        scale=wc[:, col : col + 1],
+                    )
+            for m in range(MT):
+                tabp = accp.tile([P, 512], F32, name="acc")
+                nc.tensor.matmul(
+                    out=tabp[:],
+                    lhsT=cst[:, m, :],
+                    rhs=sel[:].rearrange("p t j i e -> p (t j i e)"),
+                    start=True,
+                    stop=True,
                 )
-            tabs[nm] = tab
+                nc.scalar.copy(out=tabs_all[:, m, :, :, :, :].rearrange("p t j i e -> p (t j i e)"), in_=tabp[:])
+
+        tabs = {"q": 0, "k": 1}
+        build_tables()
 
         def mx_tiles(nm):
             codes = const.tile([P, 4, 512], U32, name="codes_" + nm, align_bytes=64)
@@ -130,8 +150,9 @@ def tile_slidingcacheattention_pa_kernel(
             for r in range(4):
                 t = deq.tile([P, K], BF16, name="wq_bf", align_bytes=64)
                 tiles.append(t)
-            width = 512 if c == 0 else K
-            for k0 in range(0, K, width):
+            widths = CFG["d0"] if c == 0 else [K]
+            for n, width in enumerate(widths):
+                k0 = sum(widths[:n])
                 for r in range(4):
                     nc.vector.tensor_tensor(
                         out=tiles[r][:, k0 : k0 + width],
@@ -192,7 +213,7 @@ def tile_slidingcacheattention_pa_kernel(
             nc.vector.tensor_tensor(
                 out=mm[:],
                 in0=acc[:].rearrange("p (h i j) -> p j h i", h=4, j=2).unsqueeze(4).to_broadcast([P, 2, 4, 64, 2]),
-                in1=tabs[st["nm"]][:, m, :, :, :].unsqueeze(2).to_broadcast([P, 2, 4, 64, 2]),
+                in1=tabs_all[:, m, tabs[st["nm"]], :, :, :].unsqueeze(2).to_broadcast([P, 2, 4, 64, 2]),
                 op=ALU.mult,
             )
             for h in range(4):
@@ -209,8 +230,18 @@ def tile_slidingcacheattention_pa_kernel(
             st["src"].append(r)
             if who == "g":
                 pair_sum(nc.gpsimd, r, mm)
+            elif who == "d":
+                nc.gpsimd.dma_start(
+                    out=mm[:, 0, :, :, :].rearrange("p h i e -> p (h i e)"),
+                    in_=mm[:, 1, :, :, :].rearrange("p h i e -> p (h i e)"),
+                    accum_op=ALU.add,
+                )
+                st["src"][m] = mm[:, 0, :, :, :].rearrange("p h i e -> p h (i e)")
             elif who == "p":
-                ps = psp.tile([P, 4, D], F32, name="ps" if CFG["ps"] else "tp")
+                if CFG["ps_acc"]:
+                    ps = accp.tile([P, 4, D], F32, name="acc")
+                else:
+                    ps = psp.tile([P, 4, D], F32, name="ps" if CFG["ps"] else "tp")
                 for j in range(2):
                     nc.tensor.matmul(
                         out=ps[:].rearrange("p h d -> p (h d)"),
@@ -292,8 +323,10 @@ def tile_slidingcacheattention_pa_kernel(
 
         q_bf = {0: dequant(0)}
         xmx = mx_tiles("x")
-        for m in (0, 2):
-            quantize(turn_quantize([(x_sb[m + a], g) for a in range(2) for g in range(PASSES)], xmx, m), xmx, m)
+        gx = [turn_quantize([(x_sb[m + a], g) for a in range(2) for g in range(PASSES)], xmx, m) for m in (0, 2)]
+        if not CFG["qx_late"]:
+            quantize(gx[0], xmx, 0)
+            quantize(gx[1], xmx, 2)
         wv_sb = load_bf16(Wv, "xv_sb")
 
         order = CFG["order"]
@@ -312,8 +345,12 @@ def tile_slidingcacheattention_pa_kernel(
             if nm == "q" and next_q < 4 and not CFG["d_late"]:
                 q_bf[next_q] = dequant(next_q)
                 next_q += 1
-            quantize(gs[0], wmx, 0)
-            quantize(gs[1], wmx, 2)
+            if i == 0 and CFG["qx_late"]:
+                quantize(gx[0], xmx, 0)
+                quantize(gx[1], xmx, 2)
+            if not CFG["q_late"][i]:
+                quantize(gs[0], wmx, 0)
+                quantize(gs[1], wmx, 2)
             last = i == len(order) - 1
             st = {
                 "nm": nm,
@@ -329,8 +366,14 @@ def tile_slidingcacheattention_pa_kernel(
             if nm != "v":
                 ss = epi.tile([P, 16], F32, name="ss")
                 st["ss"] = ss
+            if CFG["q_late"][i]:
+                for m in range(MT):
+                    if prev is not None:
+                        finish(prev, m)
+                quantize(gs[0], wmx, 0)
+                quantize(gs[1], wmx, 2)
             for m in range(MT):
-                if prev is not None:
+                if prev is not None and not CFG["q_late"][i]:
                     finish(prev, m)
                 if last and CFG["last_tp"]:
                     st["acc"].append(multiply(wmx, m, tpp, "tp"))

@@ -58,10 +58,11 @@ def tile_slidingcacheattention_pa_kernel(
         wq_view = Wq_bytes.rearrange("(c r p) k -> c p r k", p=P, r=4)
         qbytes = []
 
-        def load_scale(j):
-            nc.sync.dma_start(
-                out=scale_bc[:, 512 * j : 512 * (j + 1)], in_=Wq_scale[0, 512 * j : 512 * (j + 1)].partition_broadcast(P)
-            )
+        s_col = const.tile([P, K // P], F32, name="s_col")
+
+        def load_scale():
+            with nc.allow_non_contiguous_dma(reason="2048 scales, one to a partition and column"):
+                nc.sync.dma_start(out=s_col[:], in_=Wq_scale.rearrange("o (j p) -> p (o j)", p=P))
 
         def load_bytes(c, pieces):
             qb = rows.tile([P, 4, K], U8, name="qbytes%d" % (c % 2))
@@ -78,6 +79,8 @@ def tile_slidingcacheattention_pa_kernel(
                 tiles.append(t)
             return tiles
 
+        load_scale()
+        load_bytes(0, [(0, 2), (2, 4)])
         cs_sb = const.tile([P, MT, 2, 64], BF16, name="cs_sb")
         nc.sync.dma_start(out=cs_sb[:, :, 0, :], in_=freqs_cos.rearrange("(m p) i -> p m i", p=P))
         nc.sync.dma_start(out=cs_sb[:, :, 1, :], in_=freqs_sin.rearrange("(m p) i -> p m i", p=P))
@@ -87,10 +90,6 @@ def tile_slidingcacheattention_pa_kernel(
             for half in range(2):
                 nc.sync.dma_start(out=t[64 * half : 64 * (half + 1), :], in_=w.rearrange("(i j) -> i j", j=2))
             wc_bf[nm] = t
-        load_scale(0)
-        load_bytes(0, [(0, 2), (2, 4)])
-        for j in range(1, 4):
-            load_scale(j)
         x_sb = load_bf16(x[0], "xv_sb")
         load_bytes(1, [(0, 4)])
         wk_sb = load_bf16(Wk, "wk_sb")
@@ -105,6 +104,14 @@ def tile_slidingcacheattention_pa_kernel(
         make_identity(nc, ident[:])
         identb = const.tile([P, P], BF16, name="identb")
         make_identity(nc, identb[:])
+
+        def spread_scales():
+            for b in range(4):
+                sp = accp.tile([P, 512], F32, name="acc")
+                for a in range(4):
+                    j = 4 * b + a
+                    nc.tensor.transpose(sp[:, 128 * a : 128 * (a + 1)], s_col[:, j : j + 1].to_broadcast([P, P]), ident[:])
+                nc.scalar.copy(out=scale_bc[:, 512 * b : 512 * (b + 1)], in_=sp[:])
 
         tabs_all = const.tile([P, MT, 2, 2, 64, 2], F32, name="tabs_all")
 
@@ -138,7 +145,9 @@ def tile_slidingcacheattention_pa_kernel(
                 nc.scalar.copy(out=tabs_all[:, m, :, :, :, :].rearrange("p t j i e -> p (t j i e)"), in_=tabp[:])
 
         tabs = {"q": 0, "k": 1}
-        build_tables()
+        with tc.manual_schedule(engines={mybir.EngineType.Activation, mybir.EngineType.PE}):
+            spread_scales()
+            build_tables()
 
         def mx_tiles(nm):
             codes = const.tile([P, 4, 512], U32, name="codes_" + nm, align_bytes=64)

@@ -22,11 +22,11 @@ EPS = 1e-6
 FLOPS = 2 * 512 * 2048 * 3072
 
 CFG = {
-    "order": [("q", 0), ("k", 0), ("q", 1), ("q", 2), ("v", 0), ("q", 3)],
-    "sums": ["ggvv", "ggvv", "ggvv", "ggvv", "", "ggvv"],
+    "order": [("q", 0), ("k", 0), ("v", 0), ("q", 1), ("q", 2), ("q", 3)],
+    "sums": ["ggvv", "ggvv", "", "ggvv", "ggvv", "ggvv"],
     "last_tp": False,
     "vscale": [0, 0, 0, 0, 0, 0],
-    "fine": [False, False, False, False, False, True],
+    "fine": [False, False, False, True, True, True],
     "tp": 4,
     "d0": [512, 512, 1024],
     "ps": 0,
@@ -260,10 +260,8 @@ def tile_slidingcacheattention_pa_kernel(
                         stop=(j == 1),
                     )
                 st["src"][m] = ps
-            elif st["fine"]:
-                pair_sum(nc.vector, r, mm)
             else:
-                st["late"].append((r, mm))
+                st["late"].append((r, mm, m))
 
         def pair_sum(eng, r, mm):
             eng.tensor_tensor(
@@ -278,7 +276,7 @@ def tile_slidingcacheattention_pa_kernel(
             nc.scalar.activation(
                 out=rstd[:], in_=st["ss"][:], func=ACT.Abs_reciprocal_sqrt, bias=eps_t[:], scale=1.0 / D
             )
-            for r, mm in st["late"]:
+            for r, mm, m in st["late"]:
                 pair_sum(nc.vector, r, mm)
             for m in range(MT):
                 r = st["r"][m]
@@ -327,8 +325,19 @@ def tile_slidingcacheattention_pa_kernel(
                 plain_out(st, m)
             else:
                 rope_a(st, m)
-                if st["fine"]:
+                if st["fine"] and st["sums"][m] == "g":
                     rope_c(st, m)
+
+        def close(st):
+            if st["nm"] == "v":
+                return
+            if not st["fine"]:
+                rope_b(st)
+                return
+            for r, mm, m in st["late"]:
+                pair_sum(nc.vector, r, mm)
+            for r, mm, m in st["late"]:
+                rope_c(st, m)
 
         q_bf = {0: dequant(0)}
         xmx = mx_tiles("x")
@@ -388,11 +397,12 @@ def tile_slidingcacheattention_pa_kernel(
                     st["acc"].append(multiply(wmx, m, tpp, "tp"))
                 else:
                     st["acc"].append(multiply(wmx, m, accp, "acc"))
-            if prev is not None and prev["nm"] != "v" and not prev["fine"]:
-                rope_b(prev)
+            if prev is not None:
+                close(prev)
             if nm == "q" and next_q < 4 and CFG["d_late"]:
                 q_bf[next_q] = dequant(next_q)
                 next_q += 1
             prev = st
         for m in range(MT):
             finish(prev, m)
+        close(prev)

@@ -60,9 +60,11 @@ def tile_slidingcacheattention_pa_kernel(
 
         s_col = const.tile([P, K // P], F32, name="s_col")
 
+        s_row = const.tile([P, P], F32, name="s_row")
+        nc.vector.memset(s_row[:], 0.0)
+
         def load_scale():
-            with nc.allow_non_contiguous_dma(reason="2048 scales, one to a partition and column"):
-                nc.sync.dma_start(out=s_col[:], in_=Wq_scale.rearrange("o (j p) -> p (o j)", p=P))
+            nc.sync.dma_start(out=s_row[0 : K // P, :], in_=Wq_scale.rearrange("o (j p) -> (o j) p", p=P))
 
         def load_bytes(c, pieces):
             qb = rows.tile([P, 4, K], U8, name="qbytes%d" % (c % 2))
@@ -106,6 +108,9 @@ def tile_slidingcacheattention_pa_kernel(
         make_identity(nc, identb[:])
 
         def spread_scales():
+            colp = accp.tile([P, P], F32, name="acc")
+            nc.tensor.transpose(colp[:], s_row[:], ident[:])
+            nc.scalar.copy(out=s_col[:], in_=colp[:, 0 : K // P])
             for b in range(4):
                 sp = accp.tile([P, 512], F32, name="acc")
                 for a in range(4):

@@ -24,9 +24,11 @@ FLOPS = 2 * 512 * 2048 * 3072
 CFG = {
     "order": [("q", 0), ("k", 0), ("v", 0), ("q", 1), ("q", 2), ("q", 3)],
     "sums": ["ggvv", "ggvv", "", "ggvv", "ggvv", "ggvv"],
-    "last_tp": False,
+    "last_tp": True,
     "vscale": [0, 0, 0, 0, 0, 0],
     "fine": [False, False, False, True, True, True],
+    "deq_at": [True, True, False, False, True, False],
+    "vtail": [2],
     "tp": 4,
     "d0": [512, 512, 1024],
     "ps": 0,
@@ -238,6 +240,16 @@ def tile_slidingcacheattention_pa_kernel(
                     func=ACT.Square,
                     accum_out=st["ss"][:, 4 * m + h : 4 * m + h + 1],
                 )
+            if st["fine"]:
+                rstd = epi.tile([P, 4], F32, name="rstd4", bufs=4)
+                nc.scalar.activation(
+                    out=rstd[:],
+                    in_=st["ss"][:, 4 * m : 4 * m + 4],
+                    func=ACT.Abs_reciprocal_sqrt,
+                    bias=eps_t[:],
+                    scale=1.0 / D,
+                )
+                st["rstd"].append(rstd)
             r = epi.tile([P, 4, D], F32, name="r", bufs=CFG["r"])
             st["r"].append(r)
             who = st["sums"][m]
@@ -302,19 +314,14 @@ def tile_slidingcacheattention_pa_kernel(
                 )
 
         def rope_c(st, m):
-            rstd = epi.tile([P, 4], F32, name="rstd4", bufs=4)
-            nc.scalar.activation(
-                out=rstd[:],
-                in_=st["ss"][:, 4 * m : 4 * m + 4],
-                func=ACT.Abs_reciprocal_sqrt,
-                bias=eps_t[:],
-                scale=1.0 / D,
-            )
+            rstd = st["rstd"][m]
             r = st["r"][m]
-            for h in range(4):
-                if m >= MT - st["vscale"]:
-                    nc.vector.tensor_scalar_mul(out=r[:, h, :], in0=st["src"][m][:, h, :], scalar1=rstd[:, h : h + 1])
-                else:
+            if st["last"] and m in CFG["vtail"]:
+                nc.vector.tensor_tensor(
+                    out=r[:], in0=r[:], in1=rstd[:].unsqueeze(2).to_broadcast([P, 4, D]), op=ALU.mult
+                )
+            else:
+                for h in range(4):
                     nc.scalar.activation(
                         out=r[:, h, :], in_=st["src"][m][:, h, :], func=ACT.Copy, scale=rstd[:, h : h + 1]
                     )
@@ -365,7 +372,7 @@ def tile_slidingcacheattention_pa_kernel(
             else:
                 wmx, gs = prepare_w(wv_sb, "v")
                 dst = out_2[0]
-            if nm == "q" and next_q < 4 and not CFG["d_late"]:
+            if CFG["deq_at"][i]:
                 q_bf[next_q] = dequant(next_q)
                 next_q += 1
             if i == 0 and CFG["qx_late"]:
@@ -381,6 +388,8 @@ def tile_slidingcacheattention_pa_kernel(
                 "acc": [],
                 "r": [],
                 "late": [],
+                "rstd": [],
+                "last": last,
                 "src": [],
                 "sums": CFG["sums"][i],
                 "fine": CFG["fine"][i],

from contextlib import ExitStack

import concourse.mybir as mybir
from concourse.masks import make_identity

F32 = mybir.dt.float32
BF16 = mybir.dt.bfloat16
U32 = mybir.dt.uint32
U8 = mybir.dt.uint8
FP8 = mybir.dt.float8_e4m3fn
FP8X4 = mybir.dt.float8_e4m3fn_x4
ALU = mybir.AluOpType
ACT = mybir.ActivationFunctionType

P = 128
K = 2048
PASSES = 4
MT = 4
D = 128
EPS = 1e-6

FLOPS = 2 * 512 * 2048 * 3072

CFG = {
    "order": [("q", 0), ("k", 0), ("v", 0), ("q", 1), ("q", 2), ("q", 3)],
    "sums": ["ggvv", "ggvv", "", "ggvv", "ggvv", "ggvv"],
    "last_tp": True,
    "vscale": [0, 0, 0, 0, 0, 0],
    "fine": [False, False, False, True, True, True],
    "deq_at": [True, True, False, False, True, False],
    "vtail": [2],
    "tp": 4,
    "d0": [512, 512, 1024],
    "ps": 0,
    "ps_acc": False,
    "acc": 4,
    "mm": 3,
    "r": 8,
    "d_late": False,
    "qx_late": False,
    "q_late": [False] * 6,
}


def tile_slidingcacheattention_pa_kernel(
    tc, x, freqs_cos, freqs_sin, Wq_bytes, Wq_scale, Wk, Wv, wq_norm, wk_norm, out_0, out_1, out_2
):
    nc = tc.nc
    with ExitStack() as ctx:
        const = ctx.enter_context(tc.tile_pool(name="const", bufs=1))
        rows = ctx.enter_context(tc.tile_pool(name="rows", bufs=1))
        deq = ctx.enter_context(tc.tile_pool(name="deq", bufs=8))
        grp = ctx.enter_context(tc.tile_pool(name="grp", bufs=4))
        epi = ctx.enter_context(tc.tile_pool(name="epi", bufs=2))
        tpp = ctx.enter_context(tc.psum_pool(name="tpp", bufs=CFG["tp"]))
        accp = ctx.enter_context(tc.psum_pool(name="accp", bufs=CFG["acc"]))
        psp = ctx.enter_context(tc.psum_pool(name="psp", bufs=CFG["ps"])) if CFG["ps"] else tpp

        scale_bc = const.tile([P, K], F32, name="scale_bc")
        wq_view = Wq_bytes.rearrange("(c r p) k -> c p r k", p=P, r=4)
        qbytes = []

        s_col = const.tile([P, K // P], F32, name="s_col")

        s_row = const.tile([P, P], F32, name="s_row")
        nc.vector.memset(s_row[:], 0.0)

        def load_scale():
            nc.sync.dma_start(out=s_row[0 : K // P, :], in_=Wq_scale.rearrange("o (j p) -> (o j) p", p=P))

        def load_bytes(c, pieces):
            qb = rows.tile([P, 4, K], U8, name="qbytes%d" % (c % 2))
            for a, b in pieces:
                nc.sync.dma_start(out=qb[:, a:b, :], in_=wq_view[c][:, a:b, :])
            qbytes.append(qb)

        def load_bf16(src, nm):
            view = src.rearrange("(r p) k -> p r k", p=P)
            tiles = []
            for r in range(4):
                t = rows.tile([P, K], BF16, name="%s%d" % (nm, r))
                nc.sync.dma_start(out=t[:], in_=view[:, r, :])
                tiles.append(t)
            return tiles

        load_scale()
        load_bytes(0, [(0, 2), (2, 4)])
        cs_sb = const.tile([P, MT, 2, 64], BF16, name="cs_sb")
        nc.sync.dma_start(out=cs_sb[:, :, 0, :], in_=freqs_cos.rearrange("(m p) i -> p m i", p=P))
        nc.sync.dma_start(out=cs_sb[:, :, 1, :], in_=freqs_sin.rearrange("(m p) i -> p m i", p=P))
        wc_bf = {}
        for nm, w in (("q", wq_norm), ("k", wk_norm)):
            t = const.tile([P, 2], BF16, name="wc_bf_" + nm)
            for half in range(2):
                nc.sync.dma_start(out=t[64 * half : 64 * (half + 1), :], in_=w.rearrange("(i j) -> i j", j=2))
            wc_bf[nm] = t
        x_sb = load_bf16(x[0], "xv_sb")
        load_bytes(1, [(0, 4)])
        wk_sb = load_bf16(Wk, "wk_sb")

        one = const.tile([P, 1], F32, name="one")
        nc.vector.memset(one[:], 1.0)
        eps_t = const.tile([P, 1], F32, name="eps_t")
        nc.vector.memset(eps_t[:], EPS)
        warm = const.tile([P, 1], F32, name="warm")
        nc.scalar.activation(out=warm[:], in_=one[:], func=ACT.Abs_reciprocal_sqrt)
        ident = const.tile([P, P], F32, name="ident")
        make_identity(nc, ident[:])
        identb = const.tile([P, P], BF16, name="identb")
        make_identity(nc, identb[:])

        def spread_scales():
            colp = accp.tile([P, P], F32, name="acc")
            nc.tensor.transpose(colp[:], s_row[:], ident[:])
            nc.scalar.copy(out=s_col[:], in_=colp[:, 0 : K // P])
            for b in range(4):
                sp = accp.tile([P, 512], F32, name="acc")
                for a in range(4):
                    j = 4 * b + a
                    nc.tensor.transpose(sp[:, 128 * a : 128 * (a + 1)], s_col[:, j : j + 1].to_broadcast([P, P]), ident[:])
                nc.scalar.copy(out=scale_bc[:, 512 * b : 512 * (b + 1)], in_=sp[:])

        tabs_all = const.tile([P, MT, 2, 2, 64, 2], F32, name="tabs_all")

        def build_tables():
            cstp = accp.tile([P, MT, P], BF16, name="acc")
            for m in range(MT):
                nc.tensor.transpose(cstp[:, m, :], cs_sb[:, m, :, :].rearrange("p c i -> p (c i)"), identb[:])
            cst = const.tile([P, MT, P], BF16, name="cst")
            nc.scalar.copy(out=cst[:], in_=cstp[:])
            sel = const.tile([P, 2, 2, 64, 2], BF16, name="sel")
            for t, nm in enumerate(("q", "k")):
                wc = const.tile([P, 3], F32, name="wc_" + nm)
                nc.scalar.copy(out=wc[:, 0:2], in_=wc_bf[nm][:])
                nc.scalar.activation(out=wc[:, 2:3], in_=wc_bf[nm][:, 1:2], func=ACT.Copy, scale=-1.0)
                for j, e, c, col in ((0, 0, 0, 0), (0, 1, 1, 0), (1, 0, 1, 2), (1, 1, 0, 1)):
                    nc.scalar.activation(
                        out=sel[:, t, j, :, e],
                        in_=identb[:, 64 * c : 64 * (c + 1)],
                        func=ACT.Copy,
                        scale=wc[:, col : col + 1],
                    )
            for m in range(MT):
                tabp = accp.tile([P, 512], F32, name="acc")
                nc.tensor.matmul(
                    out=tabp[:],
                    lhsT=cst[:, m, :],
                    rhs=sel[:].rearrange("p t j i e -> p (t j i e)"),
                    start=True,
                    stop=True,
                )
                nc.scalar.copy(out=tabs_all[:, m, :, :, :, :].rearrange("p t j i e -> p (t j i e)"), in_=tabp[:])

        tabs = {"q": 0, "k": 1}
        with tc.manual_schedule(engines={mybir.EngineType.Activation, mybir.EngineType.PE}):
            spread_scales()
            build_tables()

        def mx_tiles(nm):
            codes = const.tile([P, 4, 512], U32, name="codes_" + nm, align_bytes=64)
            scl = const.tile([P, 4, 512], U8, name="scl_" + nm, align_bytes=64)
            return codes, scl

        def dequant(c):
            tiles = []
            for r in range(4):
                t = deq.tile([P, K], BF16, name="wq_bf", align_bytes=64)
                tiles.append(t)
            widths = CFG["d0"] if c == 0 else [K]
            for n, width in enumerate(widths):
                k0 = sum(widths[:n])
                for r in range(4):
                    nc.vector.tensor_tensor(
                        out=tiles[r][:, k0 : k0 + width],
                        in0=qbytes[c][:, r, k0 : k0 + width].bitcast(FP8),
                        in1=scale_bc[:, k0 : k0 + width],
                        op=ALU.mult,
                    )
            if c + 2 < 4:
                load_bytes(c + 2, [(0, 4)])
            return tiles

        def turn_quantize(blocks, mx, j):
            grouped = grp.tile([P, 1024, 4], BF16, name="grouped", align_bytes=64)
            for b in range(4):
                tp = tpp.tile([P, 2, 256], F32, name="tp")
                for r2 in range(2):
                    t, g = blocks[2 * b + r2]
                    words = t[:].bitcast(F32)
                    for u in range(2):
                        nc.tensor.transpose(
                            tp[:, u, 128 * r2 : 128 * (r2 + 1)], words[:, 256 * g + u : 256 * (g + 1) : 2], ident[:]
                        )
                nc.scalar.copy(
                    out=grouped[:, 256 * b : 256 * (b + 1), :].bitcast(F32), in_=tp[:].rearrange("p u c -> p c u")
                )
            return grouped

        def quantize(grouped, mx, j):
            nc.vector.quantize_mx(
                out=mx[0][:, j : j + 2, :].rearrange("p j c -> p (j c)").bitcast(FP8X4),
                scales=mx[1][:, j : j + 2, :].rearrange("p j c -> p (j c)"),
                in_=grouped[:].rearrange("p c t -> p (c t)"),
            )

        def prepare_w(tiles, nm):
            mx = mx_tiles(nm)
            gs = [turn_quantize([(tiles[r], g + a) for a in range(2) for r in range(4)], mx, g) for g in (0, 2)]
            return mx, gs

        def multiply(wmx, m, pool, nm):
            acc = pool.tile([P, 512], F32, name=nm)
            for g in range(PASSES):
                tok = slice(128 * g, 128 * (g + 1))
                nc.tensor.matmul_mx(
                    out=acc[:],
                    lhsT=xmx[0][:, m, tok].bitcast(FP8X4),
                    lhsT_scale=xmx[1][:, m, tok],
                    rhs=wmx[0][:, g, :].bitcast(FP8X4),
                    rhs_scale=wmx[1][:, g, :],
                    start=(g == 0),
                    stop=(g == PASSES - 1),
                )
            return acc

        def rope_a(st, m):
            acc = st["acc"][m]
            mm = epi.tile([P, 2, 4, 64, 2], F32, name="mm", bufs=CFG["mm"])
            nc.vector.tensor_tensor(
                out=mm[:],
                in0=acc[:].rearrange("p (h i j) -> p j h i", h=4, j=2).unsqueeze(4).to_broadcast([P, 2, 4, 64, 2]),
                in1=tabs_all[:, m, tabs[st["nm"]], :, :, :].unsqueeze(2).to_broadcast([P, 2, 4, 64, 2]),
                op=ALU.mult,
            )
            for h in range(4):
                junk = epi.tile([P, D], BF16, name="junk")
                nc.scalar.activation(
                    out=junk[:],
                    in_=acc[:, 128 * h : 128 * (h + 1)],
                    func=ACT.Square,
                    accum_out=st["ss"][:, 4 * m + h : 4 * m + h + 1],
                )
            if st["fine"]:
                rstd = epi.tile([P, 4], F32, name="rstd4", bufs=4)
                nc.scalar.activation(
                    out=rstd[:],
                    in_=st["ss"][:, 4 * m : 4 * m + 4],
                    func=ACT.Abs_reciprocal_sqrt,
                    bias=eps_t[:],
                    scale=1.0 / D,
                )
                st["rstd"].append(rstd)
            r = epi.tile([P, 4, D], F32, name="r", bufs=CFG["r"])
            st["r"].append(r)
            who = st["sums"][m]
            st["src"].append(r)
            if who == "g":
                pair_sum(nc.gpsimd, r, mm)
            elif who == "d":
                nc.gpsimd.dma_start(
                    out=mm[:, 0, :, :, :].rearrange("p h i e -> p (h i e)"),
                    in_=mm[:, 1, :, :, :].rearrange("p h i e -> p (h i e)"),
                    accum_op=ALU.add,
                )
                st["src"][m] = mm[:, 0, :, :, :].rearrange("p h i e -> p h (i e)")
            elif who == "p":
                if CFG["ps_acc"]:
                    ps = accp.tile([P, 4, D], F32, name="acc")
                else:
                    ps = psp.tile([P, 4, D], F32, name="ps" if CFG["ps"] else "tp")
                for j in range(2):
                    nc.tensor.matmul(
                        out=ps[:].rearrange("p h d -> p (h d)"),
                        lhsT=ident[:],
                        rhs=mm[:, j, :, :, :].rearrange("p h i e -> p (h i e)"),
                        start=(j == 0),
                        stop=(j == 1),
                    )
                st["src"][m] = ps
            else:
                st["late"].append((r, mm, m))

        def pair_sum(eng, r, mm):
            eng.tensor_tensor(
                out=r[:].rearrange("p h d -> p (h d)"),
                in0=mm[:, 0, :, :, :].rearrange("p h i e -> p (h i e)"),
                in1=mm[:, 1, :, :, :].rearrange("p h i e -> p (h i e)"),
                op=ALU.add,
            )

        def rope_b(st):
            rstd = epi.tile([P, 16], F32, name="rstd")
            nc.scalar.activation(
                out=rstd[:], in_=st["ss"][:], func=ACT.Abs_reciprocal_sqrt, bias=eps_t[:], scale=1.0 / D
            )
            for r, mm, m in st["late"]:
                pair_sum(nc.vector, r, mm)
            for m in range(MT):
                r = st["r"][m]
                for h in range(4):
                    if m >= MT - st["vscale"]:
                        nc.vector.tensor_scalar_mul(
                            out=r[:, h, :], in0=st["src"][m][:, h, :], scalar1=rstd[:, 4 * m + h : 4 * m + h + 1]
                        )
                    else:
                        nc.scalar.activation(
                            out=r[:, h, :],
                            in_=st["src"][m][:, h, :],
                            func=ACT.Copy,
                            scale=rstd[:, 4 * m + h : 4 * m + h + 1],
                        )
                nc.sync.dma_start(
                    out=st["dst"][:, 128 * m : 128 * (m + 1), :].rearrange("h n d -> n h d"), in_=r[:]
                )

        def rope_c(st, m):
            rstd = st["rstd"][m]
            r = st["r"][m]
            if st["last"] and m in CFG["vtail"]:
                nc.vector.tensor_tensor(
                    out=r[:], in0=r[:], in1=rstd[:].unsqueeze(2).to_broadcast([P, 4, D]), op=ALU.mult
                )
            else:
                for h in range(4):
                    nc.scalar.activation(
                        out=r[:, h, :], in_=st["src"][m][:, h, :], func=ACT.Copy, scale=rstd[:, h : h + 1]
                    )
            nc.sync.dma_start(out=st["dst"][:, 128 * m : 128 * (m + 1), :].rearrange("h n d -> n h d"), in_=r[:])

        def plain_out(st, m):
            vsb = epi.tile([P, 4, D], F32, name="r", bufs=CFG["r"])
            nc.scalar.copy(out=vsb[:].rearrange("p h d -> p (h d)"), in_=st["acc"][m][:])
            nc.sync.dma_start(out=st["dst"][:, 128 * m : 128 * (m + 1), :].rearrange("h n d -> n h d"), in_=vsb[:])

        def finish(st, m):
            if st["nm"] == "v":
                plain_out(st, m)
            else:
                rope_a(st, m)
                if st["fine"] and st["sums"][m] == "g":
                    rope_c(st, m)

        def close(st):
            if st["nm"] == "v":
                return
            if not st["fine"]:
                rope_b(st)
                return
            for r, mm, m in st["late"]:
                pair_sum(nc.vector, r, mm)
            for r, mm, m in st["late"]:
                rope_c(st, m)

        q_bf = {0: dequant(0)}
        xmx = mx_tiles("x")
        gx = [turn_quantize([(x_sb[m + a], g) for a in range(2) for g in range(PASSES)], xmx, m) for m in (0, 2)]
        if not CFG["qx_late"]:
            quantize(gx[0], xmx, 0)
            quantize(gx[1], xmx, 2)
        wv_sb = load_bf16(Wv, "xv_sb")

        order = CFG["order"]
        next_q = 1
        prev = None
        for i, (nm, c) in enumerate(order):
            if nm == "q":
                wmx, gs = prepare_w(q_bf[c], "q%d" % c)
                dst = out_0[0, 4 * c : 4 * (c + 1), :, :]
            elif nm == "k":
                wmx, gs = prepare_w(wk_sb, "k")
                dst = out_1[0]
            else:
                wmx, gs = prepare_w(wv_sb, "v")
                dst = out_2[0]
            if CFG["deq_at"][i]:
                q_bf[next_q] = dequant(next_q)
                next_q += 1
            if i == 0 and CFG["qx_late"]:
                quantize(gx[0], xmx, 0)
                quantize(gx[1], xmx, 2)
            if not CFG["q_late"][i]:
                quantize(gs[0], wmx, 0)
                quantize(gs[1], wmx, 2)
            last = i == len(order) - 1
            st = {
                "nm": nm,
                "dst": dst,
                "acc": [],
                "r": [],
                "late": [],
                "rstd": [],
                "last": last,
                "src": [],
                "sums": CFG["sums"][i],
                "fine": CFG["fine"][i],
                "vscale": CFG["vscale"][i],
            }
            if nm != "v":
                ss = epi.tile([P, 16], F32, name="ss")
                st["ss"] = ss
            if CFG["q_late"][i]:
                for m in range(MT):
                    if prev is not None:
                        finish(prev, m)
                quantize(gs[0], wmx, 0)
                quantize(gs[1], wmx, 2)
            for m in range(MT):
                if prev is not None and not CFG["q_late"][i]:
                    finish(prev, m)
                if last and CFG["last_tp"]:
                    st["acc"].append(multiply(wmx, m, tpp, "tp"))
                else:
                    st["acc"].append(multiply(wmx, m, accp, "acc"))
            if prev is not None:
                close(prev)
            if nm == "q" and next_q < 4 and CFG["d_late"]:
                q_bf[next_q] = dequant(next_q)
                next_q += 1
            prev = st
        for m in range(MT):
            finish(prev, m)
        close(prev)
